import numpy as np
import ml_dtypes


def mxq(x, axis, fmt="e4m3"):
    dtype, down = {"e4m3": (ml_dtypes.float8_e4m3fn, 7), "e5m2": (ml_dtypes.float8_e5m2, 14)}[fmt]
    v = np.moveaxis(np.asarray(x, np.float32).astype(ml_dtypes.bfloat16).astype(np.float64), axis, -1)
    blocks = v.reshape(v.shape[:-1] + (-1, 32))
    amax = np.abs(blocks).max(-1, keepdims=True)
    byte = np.maximum(np.where(amax > 0, np.frexp(amax)[1] - 1 + 127, 0) - down, 1)
    scale = np.exp2(byte - 127.0)
    codes = (blocks / scale).astype(np.float32).astype(dtype).astype(np.float64)
    return np.moveaxis((codes * scale).reshape(v.shape), -1, axis)


WIDE = False


def mx_kscale(k):
    if not WIDE:
        return np.ones(k)
    levels = np.array([10, -10, 5, -5, 0])
    a = np.random.permutation(np.resize(levels, k // 512 * 4)).reshape(k // 512, 4)
    idx = np.arange(k)
    return np.exp2(a[idx // 512, idx % 128 // 32])


BF16 = ml_dtypes.bfloat16


def bf(x):
    return np.asarray(x, np.float32).astype(BF16)


def f64(x):
    return np.asarray(x).astype(np.float64)


B, NB, NL, NG, NK = 4096, 512, 1536, 500, 3
N2 = 2 * NB


def setup_inputs():
    s = mx_kscale(N2)
    r = s[:NB]
    return {'Volt': bf(np.random.standard_normal((B, N2)) * s),
            'Y_top': bf(np.random.standard_normal((NB, N2)) * 4.0 / np.sqrt(N2) / s[None, :] / r[:, None]),
            'Yconj_top': bf(np.random.standard_normal((NB, N2)) * 4.0 / np.sqrt(N2) / s[None, :] / r[:, None]),
            'PQ_Loads': bf(np.random.standard_normal((B, N2))),
            'PQ_Gens': bf(np.random.standard_normal((B, N2)))}


def reference(Volt, Y_top, Yconj_top, PQ_Loads, PQ_Gens):
    V = f64(Volt)
    Vq = mxq(V, 1, 'e4m3')
    YV = Vq @ mxq(f64(Y_top), 1, 'e4m3').T
    YcV = Vq @ mxq(f64(Yconj_top), 1, 'e4m3').T
    out = np.sum(V[:, :NB] * YV, axis=1) + np.sum(V[:, :NB] * YcV, axis=1)
    pq = f64(PQ_Loads) - f64(PQ_Gens)
    return out + np.sum(pq[:, :NB], axis=1) + np.sum(pq[:, NB:], axis=1)

@@ -1,0 +1,193 @@
+from contextlib import ExitStack
+
+import concourse.mybir as mybir
+from concourse.masks import make_identity
+
+F32 = mybir.dt.float32
+BF16 = mybir.dt.bfloat16
+U32 = mybir.dt.uint32
+U8 = mybir.dt.uint8
+FP8X4 = mybir.dt.float8_e4m3fn_x4
+ALU = mybir.AluOpType
+ACT = mybir.ActivationFunctionType
+AX = mybir.AxisListType
+
+P = 128
+B = 4096
+K = 1024
+NB = 512
+TILES = B // P
+CH = 4
+NCH = TILES // CH
+FLOPS = 2 * B * K * (2 * NB)
+
+PIN = False
+PQ_BUFS = 6
+S_UNITS = [4, 3, 4, 3, 4, 3, 4, 3]
+
+
+def tile_kktloss_pc_t_kernel(tc, Volt, Y_top, Yconj_top, PQ_Loads, PQ_Gens, out):
+    nc = tc.nc
+    with ExitStack() as ctx:
+        if PIN:
+            ctx.enter_context(tc.manual_schedule())
+        const = ctx.enter_context(tc.tile_pool(name="const", bufs=1))
+        big = ctx.enter_context(tc.tile_pool(name="big", bufs=8))
+        pqp = ctx.enter_context(tc.tile_pool(name="pqp", bufs=PQ_BUFS))
+        work = ctx.enter_context(tc.tile_pool(name="work", bufs=3))
+        junk = ctx.enter_context(tc.tile_pool(name="junk", bufs=2))
+        psum = ctx.enter_context(tc.psum_pool(name="psum", bufs=4))
+
+        v_view = Volt.rearrange("(p t) k -> p t k", t=TILES)
+        pl_view = PQ_Loads.rearrange("(p t) k -> p t k", t=TILES)
+        pg_view = PQ_Gens.rearrange("(p t) k -> p t k", t=TILES)
+
+        ident = const.tile([P, P], F32)
+        make_identity(nc, ident[:])
+        y_codes = const.tile([P, 4 * NB], U32, align_bytes=64)
+        y_scales = const.tile([P, 4 * NB], U8, align_bytes=64)
+        acc_e = const.tile([P, TILES], F32)
+        acc_v = const.tile([P, 2 * TILES], F32)
+        acc_s = const.tile([P, 2 * TILES], F32)
+        nc.vector.memset(acc_v[:], 0.0)
+        nc.gpsimd.memset(acc_s[:], 0.0)
+
+        v_tiles = {}
+        pq_tiles = {}
+
+        def load_y(mat, src):
+            raw = big.tile([P, CH, K], BF16, tag="v", name="yraw%d" % mat)
+            nc.sync.dma_start(out=raw[:], in_=src.rearrange("(r p) k -> p r k", p=P))
+            return raw
+
+        def load_v(n):
+            raw = big.tile([P, CH, K], BF16, tag="v", name="v%d" % n)
+            nc.sync.dma_start(out=raw[:], in_=v_view[:, n * CH:(n + 1) * CH, :])
+            v_tiles[n] = raw
+
+        def load_pq(n):
+            raw = pqp.tile([P, 2, CH, K], BF16, tag="pq", name="pq%d" % n)
+            nc.sync.dma_start(out=raw[:, 0, :, :], in_=pl_view[:, n * CH:(n + 1) * CH, :])
+            nc.sync.dma_start(out=raw[:, 1, :, :], in_=pg_view[:, n * CH:(n + 1) * CH, :])
+            pq_tiles[n] = raw
+
+        def transposes(raw, j):
+            tp = psum.tile([P, 4, P], F32, tag="tp", name="tp")
+            words = raw[:, j, :].bitcast(F32)
+            for q in range(4):
+                nc.tensor.transpose(tp[:, q, :], words[:, q * P:(q + 1) * P], ident[:])
+            return tp
+
+        y_raw = [load_y(0, Y_top), load_y(1, Yconj_top)]
+        load_v(0)
+        load_v(1)
+        load_pq(0)
+        load_v(2)
+        load_pq(1)
+        load_v(3)
+        load_pq(2)
+        load_v(4)
+        load_pq(3)
+        load_v(5)
+        load_pq(4)
+
+        for mat in range(2):
+            grp = work.tile([P, 4 * K], BF16, tag="grp", name="grpy", align_bytes=64)
+            g32 = grp[:].bitcast(F32).rearrange("p (g i u) -> p g i u", g=2, u=2)
+            for r in range(CH):
+                tp = transposes(y_raw[mat], r)
+                src = tp[:].rearrange("p (g u) b -> p g b u", u=2)
+                dst = g32[:, :, r * P:(r + 1) * P, :]
+                if r % 2 == 0:
+                    nc.scalar.copy(out=dst, in_=src)
+                else:
+                    nc.vector.tensor_copy(out=dst, in_=src)
+            for g in range(2):
+                c0 = (mat * 2 + g) * NB
+                nc.vector.quantize_mx(
+                    out=y_codes[:, c0:c0 + NB].bitcast(FP8X4),
+                    scales=y_scales[:, c0:c0 + NB],
+                    in_=grp[:, g * 4 * NB:(g + 1) * 4 * NB],
+                )
+
+        load_v(6)
+        load_pq(5)
+        load_v(7)
+
+        quant = {}
+
+        def front(n):
+            raw = v_tiles[n]
+            grp = work.tile([P, 4 * K], BF16, tag="grp", name="grpv", align_bytes=64)
+            codes = work.tile([P, K], U32, tag="codes", name="codes", align_bytes=64)
+            scales = work.tile([P, K], U8, tag="scales", name="scales", align_bytes=64)
+            tps = [transposes(raw, j) for j in range(CH)]
+            for j in range(CH):
+                dst = grp[:, j * K:(j + 1) * K].bitcast(F32).rearrange("p (g b u) -> p g b u", g=2, u=2)
+                nc.scalar.copy(out=dst, in_=tps[j][:].rearrange("p (g u) b -> p g b u", u=2))
+            for h in range(2):
+                nc.vector.quantize_mx(
+                    out=codes[:, h * 512:(h + 1) * 512].bitcast(FP8X4),
+                    scales=scales[:, h * 512:(h + 1) * 512],
+                    in_=grp[:, h * 2048:(h + 1) * 2048],
+                )
+            quant[n] = (codes, scales)
+
+        def back(n):
+            codes, scales = quant[n]
+            raw = v_tiles[n]
+            for j in range(CH):
+                acc = psum.tile([P, NB], F32, tag="acc", name="acc")
+                i = 0
+                for g in range(2):
+                    c0 = j * 256 + g * P
+                    for mat in range(2):
+                        y0 = (mat * 2 + g) * NB
+                        nc.tensor.matmul_mx(
+                            out=acc[:],
+                            lhsT=codes[:, c0:c0 + P].bitcast(FP8X4),
+                            lhsT_scale=scales[:, c0:c0 + P],
+                            rhs=y_codes[:, y0:y0 + NB].bitcast(FP8X4),
+                            rhs_scale=y_scales[:, y0:y0 + NB],
+                            start=(i == 0),
+                            stop=(i == 3),
+                        )
+                        i += 1
+                t = n * CH + j
+                je = junk.tile([P, NB], F32, tag="je", name="je")
+                nc.vector.scalar_tensor_tensor(
+                    out=je[:], in0=acc[:], scalar=1.0, in1=raw[:, j, 0:NB],
+                    op0=ALU.mult, op1=ALU.mult, accum_out=acc_e[:, t:t + 1],
+                )
+
+        def pq_sums(n):
+            raw = pq_tiles[n]
+            for u in range(2 * CH):
+                j, w = u // 2, u % 2
+                col = 2 * (n * CH + j) + w
+                sign = 1.0 if w == 0 else -1.0
+                if u < S_UNITS[n]:
+                    js = junk.tile([P, K], BF16, tag="js", name="js")
+                    nc.scalar.activation(out=js[:], in_=raw[:, w, j, :], func=ACT.Copy, scale=sign,
+                                         accum_out=acc_s[:, col:col + 1])
+                else:
+                    jv = junk.tile([P, K], BF16, tag="jv", name="jv")
+                    nc.vector.tensor_scalar(out=jv[:], in0=raw[:, w, j, :], scalar1=sign, scalar2=None,
+                                            op0=ALU.mult, op1=ALU.add, accum_out=acc_v[:, col:col + 1])
+
+        front(0)
+        for n in range(NCH):
+            if n + 1 < NCH:
+                front(n + 1)
+            back(n)
+            pq_sums(n)
+            if n + PQ_BUFS < NCH:
+                load_pq(n + PQ_BUFS)
+
+        both = const.tile([P, 2 * TILES], F32)
+        nc.vector.tensor_tensor(out=both[:], in0=acc_v[:], in1=acc_s[:], op=ALU.add)
+        pq = const.tile([P, TILES], F32)
+        nc.vector.tensor_reduce(out=pq[:], in_=both[:].rearrange("p (t w) -> p t w", w=2), axis=AX.X, op=ALU.add)
+        res = const.tile([P, TILES], F32)
+        nc.vector.tensor_tensor(out=res[:], in0=pq[:], in1=acc_e[:], op=ALU.add)
+        nc.sync.dma_start(out=out.rearrange("(p t) -> p t", t=TILES), in_=res[:])

@@ -21,9 +21,18 @@ CH = 4
 NCH = TILES // CH
 FLOPS = 2 * B * K * (2 * NB)
 
-PIN = False
-PQ_BUFS = 6
-S_UNITS = [4, 3, 4, 3, 4, 3, 4, 3]
+PIN = True
+PQ_BUFS = 5
+G_TILES = [3, 7, 11, 15, 19, 23, 27]
+TO_VECTOR = [(29, 1), (31, 1)]
+TO_SCALAR = []
+V_D = [1, 3, 3, 3, 3, 3, 3, 3]
+S_D = [0, 3, 3, 3, 3, 3, 3, 3]
+G_D = [0, 1, 1, 1, 1, 1, 1, 1]
+LOADS_TOP = ["V0a", "V0b", "L0", "V1", "V2", "G0", "L1", "V3", "G1", "L2", "V4", "G2", "L3", "V5", "G3", "L4"]
+LOADS_AFTER_Y = ["V6", "G4", "V7"]
+LOADS_AT = {2: ["L5", "G5"], 3: ["L6", "G6"], 4: ["L7", "G7a", "G7c", "G7d"]}
+SPREAD_ORDER = [1, 2, 3, 4, 0]
 
 
 def tile_kktloss_pc_t_kernel(tc, Volt, Y_top, Yconj_top, PQ_Loads, PQ_Gens, out):
@@ -38,38 +47,47 @@ def tile_kktloss_pc_t_kernel(tc, Volt, Y_top, Yconj_top, PQ_Loads, PQ_Gens, out)
         junk = ctx.enter_context(tc.tile_pool(name="junk", bufs=2))
         psum = ctx.enter_context(tc.psum_pool(name="psum", bufs=4))
 
-        v_view = Volt.rearrange("(p t) k -> p t k", t=TILES)
-        pl_view = PQ_Loads.rearrange("(p t) k -> p t k", t=TILES)
-        pg_view = PQ_Gens.rearrange("(p t) k -> p t k", t=TILES)
+        views = {
+            "V": Volt.rearrange("(p t) k -> p t k", t=TILES),
+            "L": PQ_Loads.rearrange("(p t) k -> p t k", t=TILES),
+            "G": PQ_Gens.rearrange("(p t) k -> p t k", t=TILES),
+        }
+        parts = {"": (0, 4), "a": (0, 2), "b": (2, 4), "c": (2, 3), "d": (3, 4)}
+        held = {}
+
+        def load(token):
+            kind, n, piece = token[0], int(token[1]), token[2:]
+            if (kind, n) not in held:
+                if kind == "V":
+                    held[(kind, n)] = big.tile([P, CH, K], BF16, tag="v", name="v%d" % n)
+                else:
+                    held[(kind, n)] = pqp.tile([P, CH, K], BF16, tag="pq" + kind, name="pq%s%d" % (kind, n))
+            lo, hi = parts[piece]
+            nc.sync.dma_start(out=held[(kind, n)][:, lo:hi, :], in_=views[kind][:, n * CH + lo:n * CH + hi, :])
+
+        def loads(tokens):
+            for token in tokens:
+                load(token)
+
+        y_raw = []
+        for mat, src in enumerate((Y_top, Yconj_top)):
+            raw = big.tile([P, CH, K], BF16, tag="v", name="yraw%d" % mat)
+            for r in range(CH):
+                nc.sync.dma_start(out=raw[:, r, :], in_=src[r * P:(r + 1) * P, :])
+            y_raw.append(raw)
+        loads(LOADS_TOP)
 
         ident = const.tile([P, P], F32)
         make_identity(nc, ident[:])
         y_codes = const.tile([P, 4 * NB], U32, align_bytes=64)
         y_scales = const.tile([P, 4 * NB], U8, align_bytes=64)
         acc_e = const.tile([P, TILES], F32)
-        acc_v = const.tile([P, 2 * TILES], F32)
-        acc_s = const.tile([P, 2 * TILES], F32)
+        acc_v = const.tile([P, 2, TILES], F32)
+        acc_s = const.tile([P, TILES], F32)
+        g_acc = const.tile([P, len(G_TILES), P], F32)
+        g_sum = const.tile([P, len(G_TILES)], F32)
         nc.vector.memset(acc_v[:], 0.0)
         nc.gpsimd.memset(acc_s[:], 0.0)
-
-        v_tiles = {}
-        pq_tiles = {}
-
-        def load_y(mat, src):
-            raw = big.tile([P, CH, K], BF16, tag="v", name="yraw%d" % mat)
-            nc.sync.dma_start(out=raw[:], in_=src.rearrange("(r p) k -> p r k", p=P))
-            return raw
-
-        def load_v(n):
-            raw = big.tile([P, CH, K], BF16, tag="v", name="v%d" % n)
-            nc.sync.dma_start(out=raw[:], in_=v_view[:, n * CH:(n + 1) * CH, :])
-            v_tiles[n] = raw
-
-        def load_pq(n):
-            raw = pqp.tile([P, 2, CH, K], BF16, tag="pq", name="pq%d" % n)
-            nc.sync.dma_start(out=raw[:, 0, :, :], in_=pl_view[:, n * CH:(n + 1) * CH, :])
-            nc.sync.dma_start(out=raw[:, 1, :, :], in_=pg_view[:, n * CH:(n + 1) * CH, :])
-            pq_tiles[n] = raw
 
         def transposes(raw, j):
             tp = psum.tile([P, 4, P], F32, tag="tp", name="tp")
@@ -77,19 +95,6 @@ def tile_kktloss_pc_t_kernel(tc, Volt, Y_top, Yconj_top, PQ_Loads, PQ_Gens, out)
             for q in range(4):
                 nc.tensor.transpose(tp[:, q, :], words[:, q * P:(q + 1) * P], ident[:])
             return tp
-
-        y_raw = [load_y(0, Y_top), load_y(1, Yconj_top)]
-        load_v(0)
-        load_v(1)
-        load_pq(0)
-        load_v(2)
-        load_pq(1)
-        load_v(3)
-        load_pq(2)
-        load_v(4)
-        load_pq(3)
-        load_v(5)
-        load_pq(4)
 
         for mat in range(2):
             grp = work.tile([P, 4 * K], BF16, tag="grp", name="grpy", align_bytes=64)
@@ -109,33 +114,35 @@ def tile_kktloss_pc_t_kernel(tc, Volt, Y_top, Yconj_top, PQ_Loads, PQ_Gens, out)
                     scales=y_scales[:, c0:c0 + NB],
                     in_=grp[:, g * 4 * NB:(g + 1) * 4 * NB],
                 )
+        loads(LOADS_AFTER_Y)
 
-        load_v(6)
-        load_pq(5)
-        load_v(7)
+        front = {}
 
-        quant = {}
-
-        def front(n):
-            raw = v_tiles[n]
+        def t_chunk(n):
             grp = work.tile([P, 4 * K], BF16, tag="grp", name="grpv", align_bytes=64)
             codes = work.tile([P, K], U32, tag="codes", name="codes", align_bytes=64)
             scales = work.tile([P, K], U8, tag="scales", name="scales", align_bytes=64)
-            tps = [transposes(raw, j) for j in range(CH)]
+            tps = [transposes(held[("V", n)], j) for j in range(CH)]
+            front[n] = (grp, codes, scales, tps)
+
+        def e_chunk(n):
+            grp, codes, scales, tps = front[n]
             for j in range(CH):
                 dst = grp[:, j * K:(j + 1) * K].bitcast(F32).rearrange("p (g b u) -> p g b u", g=2, u=2)
                 nc.scalar.copy(out=dst, in_=tps[j][:].rearrange("p (g u) b -> p g b u", u=2))
-            for h in range(2):
-                nc.vector.quantize_mx(
-                    out=codes[:, h * 512:(h + 1) * 512].bitcast(FP8X4),
-                    scales=scales[:, h * 512:(h + 1) * 512],
-                    in_=grp[:, h * 2048:(h + 1) * 2048],
-                )
-            quant[n] = (codes, scales)
 
-        def back(n):
-            codes, scales = quant[n]
-            raw = v_tiles[n]
+        def q_part(n, j0, j1):
+            grp, codes, scales, tps = front[n]
+            nc.vector.quantize_mx(
+                out=codes[:, j0 * 256:j1 * 256].bitcast(FP8X4),
+                scales=scales[:, j0 * 256:j1 * 256],
+                in_=grp[:, j0 * K:j1 * K],
+            )
+
+        accs = {}
+
+        def m_chunk(n):
+            grp, codes, scales, tps = front[n]
             for j in range(CH):
                 acc = psum.tile([P, NB], F32, tag="acc", name="acc")
                 i = 0
@@ -153,41 +160,119 @@ def tile_kktloss_pc_t_kernel(tc, Volt, Y_top, Yconj_top, PQ_Loads, PQ_Gens, out)
                             stop=(i == 3),
                         )
                         i += 1
-                t = n * CH + j
-                je = junk.tile([P, NB], F32, tag="je", name="je")
-                nc.vector.scalar_tensor_tensor(
-                    out=je[:], in0=acc[:], scalar=1.0, in1=raw[:, j, 0:NB],
-                    op0=ALU.mult, op1=ALU.mult, accum_out=acc_e[:, t:t + 1],
-                )
+                accs[n * CH + j] = acc
 
-        def pq_sums(n):
-            raw = pq_tiles[n]
-            for u in range(2 * CH):
-                j, w = u // 2, u % 2
-                col = 2 * (n * CH + j) + w
-                sign = 1.0 if w == 0 else -1.0
-                if u < S_UNITS[n]:
-                    js = junk.tile([P, K], BF16, tag="js", name="js")
-                    nc.scalar.activation(out=js[:], in_=raw[:, w, j, :], func=ACT.Copy, scale=sign,
-                                         accum_out=acc_s[:, col:col + 1])
-                else:
-                    jv = junk.tile([P, K], BF16, tag="jv", name="jv")
-                    nc.vector.tensor_scalar(out=jv[:], in0=raw[:, w, j, :], scalar1=sign, scalar2=None,
-                                            op0=ALU.mult, op1=ALU.add, accum_out=acc_v[:, col:col + 1])
+        def c_tile(t):
+            je = junk.tile([P, NB], F32, tag="je", name="je")
+            nc.vector.scalar_tensor_tensor(
+                out=je[:], in0=accs[t][:], scalar=1.0, in1=held[("V", t // CH)][:, t % CH, 0:NB],
+                op0=ALU.mult, op1=ALU.mult, accum_out=acc_e[:, t:t + 1],
+            )
 
-        front(0)
+        v_units = []
+        s_units = []
         for n in range(NCH):
-            if n + 1 < NCH:
-                front(n + 1)
-            back(n)
-            pq_sums(n)
-            if n + PQ_BUFS < NCH:
-                load_pq(n + PQ_BUFS)
+            for w in range(2):
+                for j in range(CH):
+                    t = n * CH + j
+                    if t in G_TILES:
+                        continue
+                    on_vector = (w == 0 and (t, w) not in TO_SCALAR) or (t, w) in TO_VECTOR
+                    if on_vector:
+                        v_units.append((t, w))
+                    else:
+                        s_units.append((t, w))
+        done = {"v": 0, "s": 0, "g": 0, "r": 0}
 
-        both = const.tile([P, 2 * TILES], F32)
-        nc.vector.tensor_tensor(out=both[:], in0=acc_v[:], in1=acc_s[:], op=ALU.add)
-        pq = const.tile([P, TILES], F32)
-        nc.vector.tensor_reduce(out=pq[:], in_=both[:].rearrange("p (t w) -> p t w", w=2), axis=AX.X, op=ALU.add)
+        def unit_src(t, w):
+            return held[("LG"[w], t // CH)][:, t % CH, :]
+
+        def d_vector(count):
+            for unused in range(count):
+                if done["v"] < len(v_units):
+                    t, w = v_units[done["v"]]
+                    done["v"] += 1
+                    jv = junk.tile([P, K], BF16, tag="jv", name="jv")
+                    nc.vector.tensor_scalar(out=jv[:], in0=unit_src(t, w), scalar1=(1.0 - 2.0 * w), scalar2=None,
+                                            op0=ALU.mult, op1=ALU.add, accum_out=acc_v[:, w, t:t + 1])
+
+        def d_scalar(count):
+            for unused in range(count):
+                if done["s"] < len(s_units):
+                    t, w = s_units[done["s"]]
+                    done["s"] += 1
+                    js = junk.tile([P, K], BF16, tag="js", name="js")
+                    nc.scalar.activation(out=js[:], in_=unit_src(t, w), func=ACT.Copy, scale=(1.0 - 2.0 * w),
+                                         accum_out=acc_s[:, t:t + 1])
+
+        def d_gpsimd(count):
+            for unused in range(count):
+                if done["g"] < len(G_TILES):
+                    slot = done["g"]
+                    t = G_TILES[slot]
+                    done["g"] += 1
+                    pl, pg = unit_src(t, 0), unit_src(t, 1)
+                    gd = junk.tile([P, K], F32, tag="gd", name="gd")
+                    nc.gpsimd.tensor_tensor(out=gd[:, 0:512], in0=pl[:, 0:512], in1=pg[:, 0:512], op=ALU.subtract)
+                    nc.gpsimd.tensor_tensor(out=gd[:, 512:K], in0=pl[:, 512:K], in1=pg[:, 512:K], op=ALU.subtract)
+                    ge = junk.tile([P, 512], F32, tag="ge", name="ge")
+                    nc.gpsimd.tensor_tensor(out=ge[:], in0=gd[:, 0:512], in1=gd[:, 512:K], op=ALU.add)
+                    gf = junk.tile([P, 256], F32, tag="gf", name="gf")
+                    nc.gpsimd.tensor_tensor(out=gf[:], in0=ge[:, 0:256], in1=ge[:, 256:512], op=ALU.add)
+                    nc.gpsimd.tensor_tensor(out=g_acc[:, slot, :], in0=gf[:, 0:P], in1=gf[:, P:256], op=ALU.add)
+
+        def g_reduce():
+            slot = done["r"]
+            done["r"] += 1
+            nc.vector.tensor_reduce(out=g_sum[:, slot:slot + 1], in_=g_acc[:, slot, :], axis=AX.X, op=ALU.add)
+
+        t_chunk(0)
+        e_chunk(0)
+        for j in range(CH):
+            q_part(0, j, j + 1)
+        for n in range(NCH):
+            loads(LOADS_AT.get(n, []))
+            more = n + 1 < NCH
+            if n == 0:
+                m_chunk(0)
+                t_chunk(1)
+            else:
+                if more:
+                    t_chunk(n + 1)
+                m_chunk(n)
+            if more:
+                e_chunk(n + 1)
+            d_scalar(S_D[n])
+            d_gpsimd(G_D[n])
+            slots = [0, 0, 0, 0, 0]
+            for i in range(V_D[n]):
+                slots[SPREAD_ORDER[i % 5]] += 1
+            d_vector(slots[0])
+            if more:
+                q_part(n + 1, 0, 2)
+            d_vector(slots[1])
+            if more:
+                q_part(n + 1, 2, 4)
+            c_tile(n * CH)
+            c_tile(n * CH + 1)
+            d_vector(slots[2])
+            c_tile(n * CH + 2)
+            d_vector(slots[3])
+            c_tile(n * CH + 3)
+            d_vector(slots[4])
+            if done["g"] - done["r"] > 1:
+                g_reduce()
+        for unused in range(len(v_units) + len(s_units)):
+            d_vector(1)
+            d_scalar(1)
+        for unused in range(len(G_TILES) - done["r"]):
+            g_reduce()
+
+        part = const.tile([P, TILES], F32)
+        nc.vector.tensor_tensor(out=part[:], in0=acc_v[:, 0, :], in1=acc_v[:, 1, :], op=ALU.add)
+        nc.vector.tensor_tensor(out=part[:], in0=part[:], in1=acc_e[:], op=ALU.add)
+        lanes = part[:].rearrange("p (n j) -> p n j", j=CH)[:, 0:len(G_TILES), 3]
+        nc.vector.tensor_tensor(out=lanes, in0=lanes, in1=g_sum[:], op=ALU.add)
         res = const.tile([P, TILES], F32)
-        nc.vector.tensor_tensor(out=res[:], in0=pq[:], in1=acc_e[:], op=ALU.add)
+        nc.vector.tensor_tensor(out=res[:], in0=part[:], in1=acc_s[:], op=ALU.add)
         nc.sync.dma_start(out=out.rearrange("(p t) -> p t", t=TILES), in_=res[:])

@@ -23,12 +23,12 @@ FLOPS = 2 * B * K * (2 * NB)
 
 PIN = True
 PQ_BUFS = 5
-G_TILES = [3, 7, 11, 15, 19, 23, 27]
+G_TILES = []
 TO_VECTOR = [(29, 1), (31, 1)]
 TO_SCALAR = []
-V_D = [1, 3, 3, 3, 3, 3, 3, 3]
-S_D = [0, 3, 3, 3, 3, 3, 3, 3]
-G_D = [0, 1, 1, 1, 1, 1, 1, 1]
+V_D = [1, 4, 4, 4, 4, 4, 4, 4]
+S_D = [0, 4, 4, 4, 4, 4, 4, 4]
+G_D = [0, 0, 0, 0, 0, 0, 0, 0]
 LOADS_TOP = ["V0a", "V0b", "L0", "V1", "V2", "G0", "L1", "V3", "G1", "L2", "V4", "G2", "L3", "V5", "G3", "L4"]
 LOADS_AFTER_Y = ["V6", "G4", "V7"]
 LOADS_AT = {2: ["L5", "G5"], 3: ["L6", "G6"], 4: ["L7", "G7a", "G7c", "G7d"]}
@@ -84,8 +84,8 @@ def tile_kktloss_pc_t_kernel(tc, Volt, Y_top, Yconj_top, PQ_Loads, PQ_Gens, out)
         acc_e = const.tile([P, TILES], F32)
         acc_v = const.tile([P, 2, TILES], F32)
         acc_s = const.tile([P, TILES], F32)
-        g_acc = const.tile([P, len(G_TILES), P], F32)
-        g_sum = const.tile([P, len(G_TILES)], F32)
+        g_acc = const.tile([P, len(G_TILES), P], F32) if G_TILES else None
+        g_sum = const.tile([P, len(G_TILES)], F32) if G_TILES else None
         nc.vector.memset(acc_v[:], 0.0)
         nc.gpsimd.memset(acc_s[:], 0.0)
 
@@ -271,8 +271,9 @@ def tile_kktloss_pc_t_kernel(tc, Volt, Y_top, Yconj_top, PQ_Loads, PQ_Gens, out)
         part = const.tile([P, TILES], F32)
         nc.vector.tensor_tensor(out=part[:], in0=acc_v[:, 0, :], in1=acc_v[:, 1, :], op=ALU.add)
         nc.vector.tensor_tensor(out=part[:], in0=part[:], in1=acc_e[:], op=ALU.add)
-        lanes = part[:].rearrange("p (n j) -> p n j", j=CH)[:, 0:len(G_TILES), 3]
-        nc.vector.tensor_tensor(out=lanes, in0=lanes, in1=g_sum[:], op=ALU.add)
+        if G_TILES:
+            lanes = part[:].rearrange("p (n j) -> p n j", j=CH)[:, 0:len(G_TILES), 3]
+            nc.vector.tensor_tensor(out=lanes, in0=lanes, in1=g_sum[:], op=ALU.add)
         res = const.tile([P, TILES], F32)
         nc.vector.tensor_tensor(out=res[:], in0=part[:], in1=acc_s[:], op=ALU.add)
         nc.sync.dma_start(out=out.rearrange("(p t) -> p t", t=TILES), in_=res[:])

@@ -23,16 +23,15 @@ FLOPS = 2 * B * K * (2 * NB)
 
 PIN = True
 PQ_BUFS = 5
-G_TILES = []
-TO_VECTOR = [(29, 1), (31, 1)]
+G_TILES = [3, 7, 11, 15, 19, 23]
+TO_VECTOR = [(31, 1)]
 TO_SCALAR = []
-V_D = [1, 4, 4, 4, 4, 4, 4, 4]
-S_D = [0, 4, 4, 4, 4, 4, 4, 4]
-G_D = [0, 0, 0, 0, 0, 0, 0, 0]
-LOADS_TOP = ["V0a", "V0b", "L0", "V1", "V2", "G0", "L1", "V3", "G1", "L2", "V4", "G2", "L3", "V5", "G3", "L4"]
-LOADS_AFTER_Y = ["V6", "G4", "V7"]
+V_SLOTS = [[0, 0, 1, 1, 1]] * 6 + [[0, 1, 1, 1, 1]] * 2
+S_D = [0, 3, 3, 3, 3, 3, 4, 4]
+G_D = [0, 1, 1, 1, 1, 1, 1, 0]
+LOADS_TOP = ["V0a", "V0b", "V1", "L0", "V2", "G0", "L1", "V3", "G1", "L2", "V4", "G2", "V5", "L3", "G3"]
+LOADS_AFTER_Y = ["V6", "L4", "G4", "V7"]
 LOADS_AT = {2: ["L5", "G5"], 3: ["L6", "G6"], 4: ["L7", "G7a", "G7c", "G7d"]}
-SPREAD_ORDER = [1, 2, 3, 4, 0]
 
 
 def tile_kktloss_pc_t_kernel(tc, Volt, Y_top, Yconj_top, PQ_Loads, PQ_Gens, out):
@@ -84,8 +83,8 @@ def tile_kktloss_pc_t_kernel(tc, Volt, Y_top, Yconj_top, PQ_Loads, PQ_Gens, out)
         acc_e = const.tile([P, TILES], F32)
         acc_v = const.tile([P, 2, TILES], F32)
         acc_s = const.tile([P, TILES], F32)
-        g_acc = const.tile([P, len(G_TILES), P], F32) if G_TILES else None
-        g_sum = const.tile([P, len(G_TILES)], F32) if G_TILES else None
+        g_tree = const.tile([P, K], F32)
+        g_sum = const.tile([P, len(G_TILES)], F32)
         nc.vector.memset(acc_v[:], 0.0)
         nc.gpsimd.memset(acc_s[:], 0.0)
 
@@ -212,19 +211,16 @@ def tile_kktloss_pc_t_kernel(tc, Volt, Y_top, Yconj_top, PQ_Loads, PQ_Gens, out)
                     t = G_TILES[slot]
                     done["g"] += 1
                     pl, pg = unit_src(t, 0), unit_src(t, 1)
-                    gd = junk.tile([P, K], F32, tag="gd", name="gd")
-                    nc.gpsimd.tensor_tensor(out=gd[:, 0:512], in0=pl[:, 0:512], in1=pg[:, 0:512], op=ALU.subtract)
-                    nc.gpsimd.tensor_tensor(out=gd[:, 512:K], in0=pl[:, 512:K], in1=pg[:, 512:K], op=ALU.subtract)
-                    ge = junk.tile([P, 512], F32, tag="ge", name="ge")
-                    nc.gpsimd.tensor_tensor(out=ge[:], in0=gd[:, 0:512], in1=gd[:, 512:K], op=ALU.add)
-                    gf = junk.tile([P, 256], F32, tag="gf", name="gf")
-                    nc.gpsimd.tensor_tensor(out=gf[:], in0=ge[:, 0:256], in1=ge[:, 256:512], op=ALU.add)
-                    nc.gpsimd.tensor_tensor(out=g_acc[:, slot, :], in0=gf[:, 0:P], in1=gf[:, P:256], op=ALU.add)
+                    nc.gpsimd.tensor_tensor(out=g_tree[:, 0:512], in0=pl[:, 0:512], in1=pg[:, 0:512], op=ALU.subtract)
+                    nc.gpsimd.tensor_tensor(out=g_tree[:, 512:K], in0=pl[:, 512:K], in1=pg[:, 512:K], op=ALU.subtract)
+                    for half in (512, 256, 128):
+                        nc.gpsimd.tensor_tensor(out=g_tree[:, 0:half], in0=g_tree[:, 0:half],
+                                                in1=g_tree[:, half:2 * half], op=ALU.add)
 
         def g_reduce():
             slot = done["r"]
             done["r"] += 1
-            nc.vector.tensor_reduce(out=g_sum[:, slot:slot + 1], in_=g_acc[:, slot, :], axis=AX.X, op=ALU.add)
+            nc.vector.tensor_reduce(out=g_sum[:, slot:slot + 1], in_=g_tree[:, 0:P], axis=AX.X, op=ALU.add)
 
         t_chunk(0)
         e_chunk(0)
@@ -233,26 +229,21 @@ def tile_kktloss_pc_t_kernel(tc, Volt, Y_top, Yconj_top, PQ_Loads, PQ_Gens, out)
         for n in range(NCH):
             loads(LOADS_AT.get(n, []))
             more = n + 1 < NCH
-            if n == 0:
-                m_chunk(0)
-                t_chunk(1)
-            else:
-                if more:
-                    t_chunk(n + 1)
-                m_chunk(n)
+            if more:
+                t_chunk(n + 1)
+            m_chunk(n)
             if more:
                 e_chunk(n + 1)
             d_scalar(S_D[n])
-            d_gpsimd(G_D[n])
-            slots = [0, 0, 0, 0, 0]
-            for i in range(V_D[n]):
-                slots[SPREAD_ORDER[i % 5]] += 1
+            slots = V_SLOTS[n]
             d_vector(slots[0])
             if more:
                 q_part(n + 1, 0, 2)
-            d_vector(slots[1])
-            if more:
                 q_part(n + 1, 2, 4)
+            if done["g"] > done["r"]:
+                g_reduce()
+            d_gpsimd(G_D[n])
+            d_vector(slots[1])
             c_tile(n * CH)
             c_tile(n * CH + 1)
             d_vector(slots[2])
@@ -260,8 +251,6 @@ def tile_kktloss_pc_t_kernel(tc, Volt, Y_top, Yconj_top, PQ_Loads, PQ_Gens, out)
             d_vector(slots[3])
             c_tile(n * CH + 3)
             d_vector(slots[4])
-            if done["g"] - done["r"] > 1:
-                g_reduce()
         for unused in range(len(v_units) + len(s_units)):
             d_vector(1)
             d_scalar(1)
@@ -271,9 +260,8 @@ def tile_kktloss_pc_t_kernel(tc, Volt, Y_top, Yconj_top, PQ_Loads, PQ_Gens, out)
         part = const.tile([P, TILES], F32)
         nc.vector.tensor_tensor(out=part[:], in0=acc_v[:, 0, :], in1=acc_v[:, 1, :], op=ALU.add)
         nc.vector.tensor_tensor(out=part[:], in0=part[:], in1=acc_e[:], op=ALU.add)
-        if G_TILES:
-            lanes = part[:].rearrange("p (n j) -> p n j", j=CH)[:, 0:len(G_TILES), 3]
-            nc.vector.tensor_tensor(out=lanes, in0=lanes, in1=g_sum[:], op=ALU.add)
+        lanes = part[:].rearrange("p (n j) -> p n j", j=CH)[:, 0:len(G_TILES), 3]
+        nc.vector.tensor_tensor(out=lanes, in0=lanes, in1=g_sum[:], op=ALU.add)
         res = const.tile([P, TILES], F32)
         nc.vector.tensor_tensor(out=res[:], in0=part[:], in1=acc_s[:], op=ALU.add)
         nc.sync.dma_start(out=out.rearrange("(p t) -> p t", t=TILES), in_=res[:])

@@ -23,15 +23,18 @@ FLOPS = 2 * B * K * (2 * NB)
 
 PIN = True
 PQ_BUFS = 5
-G_TILES = [3, 7, 11, 15, 19, 23]
-TO_VECTOR = [(31, 1)]
+G_TILES = []
+TO_VECTOR = [(29, 1), (31, 1)]
 TO_SCALAR = []
-V_SLOTS = [[0, 0, 1, 1, 1]] * 6 + [[0, 1, 1, 1, 1]] * 2
-S_D = [0, 3, 3, 3, 3, 3, 4, 4]
-G_D = [0, 1, 1, 1, 1, 1, 1, 0]
+V_D = [3, 4, 3, 4, 3, 4, 3, 4]
+A_AT = {2: 7, 4: 15, 6: 23}
+A_TILES = [7, 15, 23]
+S_D = [0, 4, 3, 4, 3, 4, 3, 4]
+G_D = [0, 0, 0, 0, 0, 0, 0, 0]
 LOADS_TOP = ["V0a", "V0b", "V1", "L0", "V2", "G0", "L1", "V3", "G1", "L2", "V4", "G2", "V5", "L3", "G3"]
 LOADS_AFTER_Y = ["V6", "L4", "G4", "V7"]
 LOADS_AT = {2: ["L5", "G5"], 3: ["L6", "G6"], 4: ["L7", "G7a", "G7c", "G7d"]}
+SPREAD_ORDER = [1, 2, 3, 4, 0]
 
 
 def tile_kktloss_pc_t_kernel(tc, Volt, Y_top, Yconj_top, PQ_Loads, PQ_Gens, out):
@@ -78,13 +81,17 @@ def tile_kktloss_pc_t_kernel(tc, Volt, Y_top, Yconj_top, PQ_Loads, PQ_Gens, out)
 
         ident = const.tile([P, P], F32)
         make_identity(nc, ident[:])
+        plus_one = const.tile([P, P], BF16)
+        make_identity(nc, plus_one[:])
+        minus_one = const.tile([P, P], BF16)
+        nc.gpsimd.tensor_scalar(out=minus_one[:], in0=plus_one[:], scalar1=-1.0, scalar2=0.0, op0=ALU.mult, op1=ALU.add)
         y_codes = const.tile([P, 4 * NB], U32, align_bytes=64)
         y_scales = const.tile([P, 4 * NB], U8, align_bytes=64)
         acc_e = const.tile([P, TILES], F32)
         acc_v = const.tile([P, 2, TILES], F32)
         acc_s = const.tile([P, TILES], F32)
-        g_tree = const.tile([P, K], F32)
-        g_sum = const.tile([P, len(G_TILES)], F32)
+        g_acc = const.tile([P, len(G_TILES), P], F32) if G_TILES else None
+        g_sum = const.tile([P, len(G_TILES)], F32) if G_TILES else None
         nc.vector.memset(acc_v[:], 0.0)
         nc.gpsimd.memset(acc_s[:], 0.0)
 
@@ -174,7 +181,7 @@ def tile_kktloss_pc_t_kernel(tc, Volt, Y_top, Yconj_top, PQ_Loads, PQ_Gens, out)
             for w in range(2):
                 for j in range(CH):
                     t = n * CH + j
-                    if t in G_TILES:
+                    if t in G_TILES or t in A_TILES:
                         continue
                     on_vector = (w == 0 and (t, w) not in TO_SCALAR) or (t, w) in TO_VECTOR
                     if on_vector:
@@ -211,16 +218,31 @@ def tile_kktloss_pc_t_kernel(tc, Volt, Y_top, Yconj_top, PQ_Loads, PQ_Gens, out)
                     t = G_TILES[slot]
                     done["g"] += 1
                     pl, pg = unit_src(t, 0), unit_src(t, 1)
-                    nc.gpsimd.tensor_tensor(out=g_tree[:, 0:512], in0=pl[:, 0:512], in1=pg[:, 0:512], op=ALU.subtract)
-                    nc.gpsimd.tensor_tensor(out=g_tree[:, 512:K], in0=pl[:, 512:K], in1=pg[:, 512:K], op=ALU.subtract)
-                    for half in (512, 256, 128):
-                        nc.gpsimd.tensor_tensor(out=g_tree[:, 0:half], in0=g_tree[:, 0:half],
-                                                in1=g_tree[:, half:2 * half], op=ALU.add)
+                    gd = junk.tile([P, K], F32, tag="gd", name="gd")
+                    nc.gpsimd.tensor_tensor(out=gd[:, 0:512], in0=pl[:, 0:512], in1=pg[:, 0:512], op=ALU.subtract)
+                    nc.gpsimd.tensor_tensor(out=gd[:, 512:K], in0=pl[:, 512:K], in1=pg[:, 512:K], op=ALU.subtract)
+                    ge = junk.tile([P, 512], F32, tag="ge", name="ge")
+                    nc.gpsimd.tensor_tensor(out=ge[:], in0=gd[:, 0:512], in1=gd[:, 512:K], op=ALU.add)
+                    gf = junk.tile([P, 256], F32, tag="gf", name="gf")
+                    nc.gpsimd.tensor_tensor(out=gf[:], in0=ge[:, 0:256], in1=ge[:, 256:512], op=ALU.add)
+                    nc.gpsimd.tensor_tensor(out=g_acc[:, slot, :], in0=gf[:, 0:P], in1=gf[:, P:256], op=ALU.add)
+
+        def a_tile(t):
+            acc = psum.tile([P, NB], F32, tag="acc", name="acc")
+            for i in range(4):
+                w, c = i // 2, i % 2
+                nc.tensor.matmul(out=acc[:], lhsT=(plus_one if w == 0 else minus_one)[:],
+                                 rhs=unit_src(t, w)[:, c * NB:(c + 1) * NB], start=(i == 0), stop=(i == 3))
+            accs[("a", t)] = acc
+
+        def r_tile(t):
+            jr = junk.tile([P, NB], F32, tag="jr", name="jr")
+            nc.scalar.activation(out=jr[:], in_=accs[("a", t)][:], func=ACT.Copy, accum_out=acc_s[:, t:t + 1])
 
         def g_reduce():
             slot = done["r"]
             done["r"] += 1
-            nc.vector.tensor_reduce(out=g_sum[:, slot:slot + 1], in_=g_tree[:, 0:P], axis=AX.X, op=ALU.add)
+            nc.vector.tensor_reduce(out=g_sum[:, slot:slot + 1], in_=g_acc[:, slot, :], axis=AX.X, op=ALU.add)
 
         t_chunk(0)
         e_chunk(0)
@@ -232,18 +254,23 @@ def tile_kktloss_pc_t_kernel(tc, Volt, Y_top, Yconj_top, PQ_Loads, PQ_Gens, out)
             if more:
                 t_chunk(n + 1)
             m_chunk(n)
+            if n in A_AT:
+                a_tile(A_AT[n])
             if more:
                 e_chunk(n + 1)
             d_scalar(S_D[n])
-            slots = V_SLOTS[n]
+            if n in A_AT:
+                r_tile(A_AT[n])
+            d_gpsimd(G_D[n])
+            slots = [0, 0, 0, 0, 0]
+            for i in range(V_D[n]):
+                slots[SPREAD_ORDER[i % 5]] += 1
             d_vector(slots[0])
             if more:
                 q_part(n + 1, 0, 2)
-                q_part(n + 1, 2, 4)
-            if done["g"] > done["r"]:
-                g_reduce()
-            d_gpsimd(G_D[n])
             d_vector(slots[1])
+            if more:
+                q_part(n + 1, 2, 4)
             c_tile(n * CH)
             c_tile(n * CH + 1)
             d_vector(slots[2])
@@ -251,17 +278,20 @@ def tile_kktloss_pc_t_kernel(tc, Volt, Y_top, Yconj_top, PQ_Loads, PQ_Gens, out)
             d_vector(slots[3])
             c_tile(n * CH + 3)
             d_vector(slots[4])
-        for unused in range(len(v_units) + len(s_units)):
-            d_vector(1)
-            d_scalar(1)
+            if done["g"] - done["r"] > 1:
+                g_reduce()
+        d_scalar(len(s_units))
+        d_vector(len(v_units) - done["v"] - len(TO_VECTOR))
+        part = const.tile([P, TILES], F32)
+        nc.vector.tensor_tensor(out=part[:], in0=acc_v[:, 0, :], in1=acc_e[:], op=ALU.add)
+        d_vector(len(TO_VECTOR))
         for unused in range(len(G_TILES) - done["r"]):
             g_reduce()
 
-        part = const.tile([P, TILES], F32)
-        nc.vector.tensor_tensor(out=part[:], in0=acc_v[:, 0, :], in1=acc_v[:, 1, :], op=ALU.add)
-        nc.vector.tensor_tensor(out=part[:], in0=part[:], in1=acc_e[:], op=ALU.add)
-        lanes = part[:].rearrange("p (n j) -> p n j", j=CH)[:, 0:len(G_TILES), 3]
-        nc.vector.tensor_tensor(out=lanes, in0=lanes, in1=g_sum[:], op=ALU.add)
+        nc.vector.tensor_tensor(out=part[:], in0=part[:], in1=acc_v[:, 1, :], op=ALU.add)
+        if G_TILES:
+            lanes = part[:].rearrange("p (n j) -> p n j", j=CH)[:, 0:len(G_TILES), 3]
+            nc.vector.tensor_tensor(out=lanes, in0=lanes, in1=g_sum[:], op=ALU.add)
         res = const.tile([P, TILES], F32)
         nc.vector.tensor_tensor(out=res[:], in0=part[:], in1=acc_s[:], op=ALU.add)
         nc.sync.dma_start(out=out.rearrange("(p t) -> p t", t=TILES), in_=res[:])

@@ -26,14 +26,14 @@ PQ_BUFS = 5
 G_TILES = []
 TO_VECTOR = [(29, 1), (31, 1)]
 TO_SCALAR = []
-V_D = [3, 4, 3, 4, 3, 4, 3, 4]
-A_AT = {2: 7, 4: 15, 6: 23}
-A_TILES = [7, 15, 23]
-S_D = [0, 4, 3, 4, 3, 4, 3, 4]
+V_D = [4, 4, 4, 4, 4, 5, 5, 5]
+A_AT = {3: 11, 6: 23}
+A_TILES = [11, 23]
+S_D = [3, 3, 4, 3, 4, 4, 4, 4]
 G_D = [0, 0, 0, 0, 0, 0, 0, 0]
-LOADS_TOP = ["V0a", "V0b", "V1", "L0", "V2", "G0", "L1", "V3", "G1", "L2", "V4", "G2", "V5", "L3", "G3"]
-LOADS_AFTER_Y = ["V6", "L4", "G4", "V7"]
-LOADS_AT = {2: ["L5", "G5"], 3: ["L6", "G6"], 4: ["L7", "G7a", "G7c", "G7d"]}
+LOADS_TOP = ["V0a", "V0b", "V1", "L0", "G0", "V2", "L1", "G1", "V3", "L2", "G2", "V4", "L3", "G3", "V5", "L4"]
+LOADS_AFTER_Y = ["V6", "G4"]
+LOADS_AT = {1: ["L5"], 2: ["L6", "G5", "V7"], 4: ["L7", "G6", "G7a", "G7c", "G7d"]}
 SPREAD_ORDER = [1, 2, 3, 4, 0]
 
 

@@ -21,7 +21,7 @@ CH = 4
 NCH = TILES // CH
 FLOPS = 2 * B * K * (2 * NB)
 
-PIN = True
+PIN = False
 PQ_BUFS = 5
 G_TILES = []
 TO_VECTOR = [(29, 1), (31, 1)]

from contextlib import ExitStack

import concourse.mybir as mybir
from concourse.masks import make_identity

F32 = mybir.dt.float32
BF16 = mybir.dt.bfloat16
U32 = mybir.dt.uint32
U8 = mybir.dt.uint8
FP8X4 = mybir.dt.float8_e4m3fn_x4
ALU = mybir.AluOpType
ACT = mybir.ActivationFunctionType
AX = mybir.AxisListType

P = 128
B = 4096
K = 1024
NB = 512
TILES = B // P
CH = 4
NCH = TILES // CH
FLOPS = 2 * B * K * (2 * NB)

PIN = False
PQ_BUFS = 5
G_TILES = []
TO_VECTOR = [(29, 1), (31, 1)]
TO_SCALAR = []
V_D = [4, 4, 4, 4, 4, 5, 5, 5]
A_AT = {3: 11, 6: 23}
A_TILES = [11, 23]
S_D = [3, 3, 4, 3, 4, 4, 4, 4]
G_D = [0, 0, 0, 0, 0, 0, 0, 0]
LOADS_TOP = ["V0a", "V0b", "V1", "L0", "G0", "V2", "L1", "G1", "V3", "L2", "G2", "V4", "L3", "G3", "V5", "L4"]
LOADS_AFTER_Y = ["V6", "G4"]
LOADS_AT = {1: ["L5"], 2: ["L6", "G5", "V7"], 4: ["L7", "G6", "G7a", "G7c", "G7d"]}
SPREAD_ORDER = [1, 2, 3, 4, 0]


def tile_kktloss_pc_t_kernel(tc, Volt, Y_top, Yconj_top, PQ_Loads, PQ_Gens, out):
    nc = tc.nc
    with ExitStack() as ctx:
        if PIN:
            ctx.enter_context(tc.manual_schedule())
        const = ctx.enter_context(tc.tile_pool(name="const", bufs=1))
        big = ctx.enter_context(tc.tile_pool(name="big", bufs=8))
        pqp = ctx.enter_context(tc.tile_pool(name="pqp", bufs=PQ_BUFS))
        work = ctx.enter_context(tc.tile_pool(name="work", bufs=3))
        junk = ctx.enter_context(tc.tile_pool(name="junk", bufs=2))
        psum = ctx.enter_context(tc.psum_pool(name="psum", bufs=4))

        views = {
            "V": Volt.rearrange("(p t) k -> p t k", t=TILES),
            "L": PQ_Loads.rearrange("(p t) k -> p t k", t=TILES),
            "G": PQ_Gens.rearrange("(p t) k -> p t k", t=TILES),
        }
        parts = {"": (0, 4), "a": (0, 2), "b": (2, 4), "c": (2, 3), "d": (3, 4)}
        held = {}

        def load(token):
            kind, n, piece = token[0], int(token[1]), token[2:]
            if (kind, n) not in held:
                if kind == "V":
                    held[(kind, n)] = big.tile([P, CH, K], BF16, tag="v", name="v%d" % n)
                else:
                    held[(kind, n)] = pqp.tile([P, CH, K], BF16, tag="pq" + kind, name="pq%s%d" % (kind, n))
            lo, hi = parts[piece]
            nc.sync.dma_start(out=held[(kind, n)][:, lo:hi, :], in_=views[kind][:, n * CH + lo:n * CH + hi, :])

        def loads(tokens):
            for token in tokens:
                load(token)

        y_raw = []
        for mat, src in enumerate((Y_top, Yconj_top)):
            raw = big.tile([P, CH, K], BF16, tag="v", name="yraw%d" % mat)
            for r in range(CH):
                nc.sync.dma_start(out=raw[:, r, :], in_=src[r * P:(r + 1) * P, :])
            y_raw.append(raw)
        loads(LOADS_TOP)

        ident = const.tile([P, P], F32)
        make_identity(nc, ident[:])
        plus_one = const.tile([P, P], BF16)
        make_identity(nc, plus_one[:])
        minus_one = const.tile([P, P], BF16)
        nc.gpsimd.tensor_scalar(out=minus_one[:], in0=plus_one[:], scalar1=-1.0, scalar2=0.0, op0=ALU.mult, op1=ALU.add)
        y_codes = const.tile([P, 4 * NB], U32, align_bytes=64)
        y_scales = const.tile([P, 4 * NB], U8, align_bytes=64)
        acc_e = const.tile([P, TILES], F32)
        acc_v = const.tile([P, 2, TILES], F32)
        acc_s = const.tile([P, TILES], F32)
        g_acc = const.tile([P, len(G_TILES), P], F32) if G_TILES else None
        g_sum = const.tile([P, len(G_TILES)], F32) if G_TILES else None
        nc.vector.memset(acc_v[:], 0.0)
        nc.gpsimd.memset(acc_s[:], 0.0)

        def transposes(raw, j):
            tp = psum.tile([P, 4, P], F32, tag="tp", name="tp")
            words = raw[:, j, :].bitcast(F32)
            for q in range(4):
                nc.tensor.transpose(tp[:, q, :], words[:, q * P:(q + 1) * P], ident[:])
            return tp

        for mat in range(2):
            grp = work.tile([P, 4 * K], BF16, tag="grp", name="grpy", align_bytes=64)
            g32 = grp[:].bitcast(F32).rearrange("p (g i u) -> p g i u", g=2, u=2)
            for r in range(CH):
                tp = transposes(y_raw[mat], r)
                src = tp[:].rearrange("p (g u) b -> p g b u", u=2)
                dst = g32[:, :, r * P:(r + 1) * P, :]
                if r % 2 == 0:
                    nc.scalar.copy(out=dst, in_=src)
                else:
                    nc.vector.tensor_copy(out=dst, in_=src)
            for g in range(2):
                c0 = (mat * 2 + g) * NB
                nc.vector.quantize_mx(
                    out=y_codes[:, c0:c0 + NB].bitcast(FP8X4),
                    scales=y_scales[:, c0:c0 + NB],
                    in_=grp[:, g * 4 * NB:(g + 1) * 4 * NB],
                )
        loads(LOADS_AFTER_Y)

        front = {}

        def t_chunk(n):
            grp = work.tile([P, 4 * K], BF16, tag="grp", name="grpv", align_bytes=64)
            codes = work.tile([P, K], U32, tag="codes", name="codes", align_bytes=64)
            scales = work.tile([P, K], U8, tag="scales", name="scales", align_bytes=64)
            tps = [transposes(held[("V", n)], j) for j in range(CH)]
            front[n] = (grp, codes, scales, tps)

        def e_chunk(n):
            grp, codes, scales, tps = front[n]
            for j in range(CH):
                dst = grp[:, j * K:(j + 1) * K].bitcast(F32).rearrange("p (g b u) -> p g b u", g=2, u=2)
                nc.scalar.copy(out=dst, in_=tps[j][:].rearrange("p (g u) b -> p g b u", u=2))

        def q_part(n, j0, j1):
            grp, codes, scales, tps = front[n]
            nc.vector.quantize_mx(
                out=codes[:, j0 * 256:j1 * 256].bitcast(FP8X4),
                scales=scales[:, j0 * 256:j1 * 256],
                in_=grp[:, j0 * K:j1 * K],
            )

        accs = {}

        def m_chunk(n):
            grp, codes, scales, tps = front[n]
            for j in range(CH):
                acc = psum.tile([P, NB], F32, tag="acc", name="acc")
                i = 0
                for g in range(2):
                    c0 = j * 256 + g * P
                    for mat in range(2):
                        y0 = (mat * 2 + g) * NB
                        nc.tensor.matmul_mx(
                            out=acc[:],
                            lhsT=codes[:, c0:c0 + P].bitcast(FP8X4),
                            lhsT_scale=scales[:, c0:c0 + P],
                            rhs=y_codes[:, y0:y0 + NB].bitcast(FP8X4),
                            rhs_scale=y_scales[:, y0:y0 + NB],
                            start=(i == 0),
                            stop=(i == 3),
                        )
                        i += 1
                accs[n * CH + j] = acc

        def c_tile(t):
            je = junk.tile([P, NB], F32, tag="je", name="je")
            nc.vector.scalar_tensor_tensor(
                out=je[:], in0=accs[t][:], scalar=1.0, in1=held[("V", t // CH)][:, t % CH, 0:NB],
                op0=ALU.mult, op1=ALU.mult, accum_out=acc_e[:, t:t + 1],
            )

        v_units = []
        s_units = []
        for n in range(NCH):
            for w in range(2):
                for j in range(CH):
                    t = n * CH + j
                    if t in G_TILES or t in A_TILES:
                        continue
                    on_vector = (w == 0 and (t, w) not in TO_SCALAR) or (t, w) in TO_VECTOR
                    if on_vector:
                        v_units.append((t, w))
                    else:
                        s_units.append((t, w))
        done = {"v": 0, "s": 0, "g": 0, "r": 0}

        def unit_src(t, w):
            return held[("LG"[w], t // CH)][:, t % CH, :]

        def d_vector(count):
            for unused in range(count):
                if done["v"] < len(v_units):
                    t, w = v_units[done["v"]]
                    done["v"] += 1
                    jv = junk.tile([P, K], BF16, tag="jv", name="jv")
                    nc.vector.tensor_scalar(out=jv[:], in0=unit_src(t, w), scalar1=(1.0 - 2.0 * w), scalar2=None,
                                            op0=ALU.mult, op1=ALU.add, accum_out=acc_v[:, w, t:t + 1])

        def d_scalar(count):
            for unused in range(count):
                if done["s"] < len(s_units):
                    t, w = s_units[done["s"]]
                    done["s"] += 1
                    js = junk.tile([P, K], BF16, tag="js", name="js")
                    nc.scalar.activation(out=js[:], in_=unit_src(t, w), func=ACT.Copy, scale=(1.0 - 2.0 * w),
                                         accum_out=acc_s[:, t:t + 1])

        def d_gpsimd(count):
            for unused in range(count):
                if done["g"] < len(G_TILES):
                    slot = done["g"]
                    t = G_TILES[slot]
                    done["g"] += 1
                    pl, pg = unit_src(t, 0), unit_src(t, 1)
                    gd = junk.tile([P, K], F32, tag="gd", name="gd")
                    nc.gpsimd.tensor_tensor(out=gd[:, 0:512], in0=pl[:, 0:512], in1=pg[:, 0:512], op=ALU.subtract)
                    nc.gpsimd.tensor_tensor(out=gd[:, 512:K], in0=pl[:, 512:K], in1=pg[:, 512:K], op=ALU.subtract)
                    ge = junk.tile([P, 512], F32, tag="ge", name="ge")
                    nc.gpsimd.tensor_tensor(out=ge[:], in0=gd[:, 0:512], in1=gd[:, 512:K], op=ALU.add)
                    gf = junk.tile([P, 256], F32, tag="gf", name="gf")
                    nc.gpsimd.tensor_tensor(out=gf[:], in0=ge[:, 0:256], in1=ge[:, 256:512], op=ALU.add)
                    nc.gpsimd.tensor_tensor(out=g_acc[:, slot, :], in0=gf[:, 0:P], in1=gf[:, P:256], op=ALU.add)

        def a_tile(t):
            acc = psum.tile([P, NB], F32, tag="acc", name="acc")
            for i in range(4):
                w, c = i // 2, i % 2
                nc.tensor.matmul(out=acc[:], lhsT=(plus_one if w == 0 else minus_one)[:],
                                 rhs=unit_src(t, w)[:, c * NB:(c + 1) * NB], start=(i == 0), stop=(i == 3))
            accs[("a", t)] = acc

        def r_tile(t):
            jr = junk.tile([P, NB], F32, tag="jr", name="jr")
            nc.scalar.activation(out=jr[:], in_=accs[("a", t)][:], func=ACT.Copy, accum_out=acc_s[:, t:t + 1])

        def g_reduce():
            slot = done["r"]
            done["r"] += 1
            nc.vector.tensor_reduce(out=g_sum[:, slot:slot + 1], in_=g_acc[:, slot, :], axis=AX.X, op=ALU.add)

        t_chunk(0)
        e_chunk(0)
        for j in range(CH):
            q_part(0, j, j + 1)
        for n in range(NCH):
            loads(LOADS_AT.get(n, []))
            more = n + 1 < NCH
            if more:
                t_chunk(n + 1)
            m_chunk(n)
            if n in A_AT:
                a_tile(A_AT[n])
            if more:
                e_chunk(n + 1)
            d_scalar(S_D[n])
            if n in A_AT:
                r_tile(A_AT[n])
            d_gpsimd(G_D[n])
            slots = [0, 0, 0, 0, 0]
            for i in range(V_D[n]):
                slots[SPREAD_ORDER[i % 5]] += 1
            d_vector(slots[0])
            if more:
                q_part(n + 1, 0, 2)
            d_vector(slots[1])
            if more:
                q_part(n + 1, 2, 4)
            c_tile(n * CH)
            c_tile(n * CH + 1)
            d_vector(slots[2])
            c_tile(n * CH + 2)
            d_vector(slots[3])
            c_tile(n * CH + 3)
            d_vector(slots[4])
            if done["g"] - done["r"] > 1:
                g_reduce()
        d_scalar(len(s_units))
        d_vector(len(v_units) - done["v"] - len(TO_VECTOR))
        part = const.tile([P, TILES], F32)
        nc.vector.tensor_tensor(out=part[:], in0=acc_v[:, 0, :], in1=acc_e[:], op=ALU.add)
        d_vector(len(TO_VECTOR))
        for unused in range(len(G_TILES) - done["r"]):
            g_reduce()

        nc.vector.tensor_tensor(out=part[:], in0=part[:], in1=acc_v[:, 1, :], op=ALU.add)
        if G_TILES:
            lanes = part[:].rearrange("p (n j) -> p n j", j=CH)[:, 0:len(G_TILES), 3]
            nc.vector.tensor_tensor(out=lanes, in0=lanes, in1=g_sum[:], op=ALU.add)
        res = const.tile([P, TILES], F32)
        nc.vector.tensor_tensor(out=res[:], in0=part[:], in1=acc_s[:], op=ALU.add)
        nc.sync.dma_start(out=out.rearrange("(p t) -> p t", t=TILES), in_=res[:])
